import numpy as np
import ml_dtypes


def mxq(x, axis, fmt="e4m3"):
    dtype, down = {"e4m3": (ml_dtypes.float8_e4m3fn, 7), "e5m2": (ml_dtypes.float8_e5m2, 14)}[fmt]
    v = np.moveaxis(np.asarray(x, np.float32).astype(ml_dtypes.bfloat16).astype(np.float64), axis, -1)
    blocks = v.reshape(v.shape[:-1] + (-1, 32))
    amax = np.abs(blocks).max(-1, keepdims=True)
    byte = np.maximum(np.where(amax > 0, np.frexp(amax)[1] - 1 + 127, 0) - down, 1)
    scale = np.exp2(byte - 127.0)
    codes = (blocks / scale).astype(np.float32).astype(dtype).astype(np.float64)
    return np.moveaxis((codes * scale).reshape(v.shape), -1, axis)


WIDE = False


def mx_kscale(k):
    if not WIDE:
        return np.ones(k)
    levels = np.array([30, -30])
    if k % 512:
        return np.exp2(np.random.permutation(np.resize(levels, k // 32))).repeat(32)
    a = np.empty((k // 512, 16))
    for p in range(k // 512):
        a[p, :8] = np.random.permutation(np.resize(levels, 8))
        for g in range(8):
            far = levels[np.abs(levels - a[p, g]) >= 10]
            a[p, g + 8] = far[np.random.randint(len(far))]
    return np.exp2(a.ravel()).repeat(32)


BF16 = ml_dtypes.bfloat16


def bf(x):
    return np.asarray(x, np.float32).astype(BF16)


def f64(x):
    return np.asarray(x).astype(np.float64)


B, T, C, H, KH, D = 4, 128, 2048, 16, 4, 128
HALF = D // 2
RMS_EPS = 1e-6


def rms_norm(v, w):
    var = np.mean(v * v, axis=-1, keepdims=True)
    return v * (1.0 / np.sqrt(var + RMS_EPS)) * w


def rotary(v, cos, sin):
    v1, v2 = v[..., :HALF], v[..., HALF:]
    return np.concatenate([v1 * cos - v2 * sin, v1 * sin + v2 * cos], axis=-1)


def setup_inputs():
    s = mx_kscale(C)
    return {"x": bf(np.random.standard_normal((B, T, C)) * s),
            "cos": bf(np.random.uniform(0.0, 1.0, (1, T, 1, HALF))),
            "sin": bf(np.random.uniform(0.0, 1.0, (1, T, 1, HALF))),
            "wq": bf(np.random.standard_normal((C, H * D)) / np.sqrt(C) / s[:, None]),
            "wk": bf(np.random.standard_normal((C, KH * D)) / np.sqrt(C) / s[:, None]),
            "q_norm_w": bf(1.0 + 0.1 * np.random.standard_normal(D)),
            "k_norm_w": bf(1.0 + 0.1 * np.random.standard_normal(D))}


def reference(x, cos, sin, wq, wk, q_norm_w, k_norm_w):
    xq = mxq(f64(x), 2, "e5m2")
    q = (xq @ mxq(f64(wq), 0, "e5m2")).reshape(B, T, H, D)
    k = (xq @ mxq(f64(wk), 0, "e5m2")).reshape(B, T, KH, D)
    q = rms_norm(q, f64(q_norm_w))
    k = rms_norm(k, f64(k_norm_w))
    q = rotary(q, f64(cos), f64(sin))
    k = rotary(k, f64(cos), f64(sin))
    return q, k

@@ -1,0 +1,281 @@
+from contextlib import ExitStack
+
+import concourse.mybir as mybir
+from concourse.masks import make_identity
+
+BATCH, T, C, H, KH, D = 4, 128, 2048, 16, 4, 128
+HALF = D // 2
+RMS_EPS = 1e-6
+FLOPS = 2 * BATCH * T * C * (H + KH) * D
+
+F32 = mybir.dt.float32
+BF16 = mybir.dt.bfloat16
+U32 = mybir.dt.uint32
+U8 = mybir.dt.uint8
+E5M2X4 = mybir.dt.float8_e5m2_x4
+ALU = mybir.AluOpType
+ACT = mybir.ActivationFunctionType
+
+P = 128
+PACK = 4
+K_PASS = P * PACK
+PASSES = C // K_PASS
+N_TILE = 512
+HEADS_PER_TILE = N_TILE // D
+COL_TILES = (H + KH) * D // N_TILE
+UNITS = COL_TILES * PASSES
+BANKS = COL_TILES * BATCH
+PREFETCH = 8
+
+
+def vector_columns(u):
+    if u < 4:
+        return 320
+    if u < 6:
+        return 256
+    return 192
+
+
+def tile_multiheadattention_pa_kernel(tc, x, cos, sin, wq, wk, q_norm_w, k_norm_w, out_0, out_1):
+    nc = tc.nc
+    x_rows = x.flatten_outer_dims()
+
+    with ExitStack() as ctx:
+        ctx.enter_context(tc.manual_schedule())
+        const = ctx.enter_context(tc.tile_pool(name="const", bufs=1))
+        wraw = ctx.enter_context(tc.tile_pool(name="wraw", bufs=1))
+        grp = ctx.enter_context(tc.tile_pool(name="grp", bufs=3))
+        wcp = ctx.enter_context(tc.tile_pool(name="wcp", bufs=6))
+        stat = ctx.enter_context(tc.tile_pool(name="stat", bufs=4))
+        epi = ctx.enter_context(tc.tile_pool(name="epi", bufs=3))
+        outp = ctx.enter_context(tc.tile_pool(name="outp", bufs=4))
+        psum = ctx.enter_context(tc.psum_pool(name="psum", bufs=8))
+
+        cs = const.tile([P, 2, HALF], BF16, name="cs")
+        gain_rows = const.tile([P, 2 * D], BF16, name="gain_rows")
+        ones = const.tile([P, P], BF16, name="ones")
+        ident = const.tile([P, P], F32, name="ident")
+        eps = const.tile([P, 1], F32, name="eps")
+        warm = const.tile([P, 1], F32, name="warm")
+        nc.gpsimd.memset(eps[:], RMS_EPS)
+        nc.gpsimd.memset(gain_rows[:], 0.0)
+        nc.gpsimd.memset(ones[:], 1.0)
+        make_identity(nc, ident[:])
+        nc.scalar.dma_start(out=gain_rows[0:1, 0:D], in_=q_norm_w.rearrange("(o d) -> o d", o=1))
+        nc.scalar.dma_start(out=gain_rows[0:1, D : 2 * D], in_=k_norm_w.rearrange("(o d) -> o d", o=1))
+        nc.scalar.dma_start(out=cs[:, 0, :], in_=cos.rearrange("a t b e -> (a t) (b e)"))
+        nc.scalar.dma_start(out=cs[:, 1, :], in_=sin.rearrange("a t b e -> (a t) (b e)"))
+        nc.scalar.activation(out=warm[:], in_=eps[:], func=ACT.Sqrt)
+
+        w_raw = {}
+        x_raw = {}
+
+        def load_unit(u):
+            n, g = divmod(u, PASSES)
+            rows = slice(g * K_PASS, (g + 1) * K_PASS)
+            if n == 0:
+                src = wk[rows, :]
+            else:
+                src = wq[rows, (n - 1) * N_TILE : n * N_TILE]
+            raw = wraw.tile([P, PACK, N_TILE], BF16, name="w_raw%d" % u)
+            nc.sync.dma_start(out=raw[:], in_=src.rearrange("(p j) w -> p j w", j=PACK))
+            w_raw[u] = raw
+
+        def load_x(m):
+            raw = wraw.tile([P, C], BF16, name="x_raw%d" % m)
+            nc.sync.dma_start(out=raw[:], in_=x_rows[m * P : (m + 1) * P, :])
+            x_raw[m] = raw
+
+        for m in range(BATCH):
+            load_unit(m)
+            load_x(m)
+        for u in range(BATCH, PREFETCH):
+            load_unit(u)
+
+        tab_a = const.tile([P, 2, D], F32, name="tab_a")
+        tab_b = const.tile([P, 2, 2, HALF], F32, name="tab_b")
+        gain_bank = psum.tile([P, N_TILE], F32, name="bank")
+        nc.tensor.matmul(out=gain_bank[:, 0 : 2 * D], lhsT=ones[:], rhs=gain_rows[:], start=True, stop=True)
+
+        def build_tables():
+            gains = gain_bank[:, 0 : 2 * D]
+            by_half = gains.rearrange("p (q two e) -> p q two e", q=2, two=2)
+            nc.vector.tensor_tensor(
+                out=tab_a[:].rearrange("p q (two e) -> p (q two) e", two=2),
+                in0=gains.rearrange("p (f e) -> p f e", e=HALF),
+                in1=cs[:, 0:1, :].to_broadcast([P, 4, HALF]),
+                op=ALU.mult,
+            )
+            nc.vector.scalar_tensor_tensor(
+                out=tab_b[:, :, 0, :],
+                in0=by_half[:, :, 1, :],
+                scalar=-1.0,
+                in1=cs[:, 1:2, :].to_broadcast([P, 2, HALF]),
+                op0=ALU.mult,
+                op1=ALU.mult,
+            )
+            nc.vector.tensor_tensor(
+                out=tab_b[:, :, 1, :],
+                in0=by_half[:, :, 0, :],
+                in1=cs[:, 1:2, :].to_broadcast([P, 2, HALF]),
+                op=ALU.mult,
+            )
+
+        x_codes = const.tile([P, BATCH, PASSES * P], U32, name="x_codes", align_bytes=64)
+        x_scales = const.tile([P, BATCH, PASSES * P], U8, name="x_scales", align_bytes=64)
+        x_grouped = {}
+
+        def transpose_x(m):
+            words = x_raw[m][:].bitcast(F32)
+            grouped = grp.tile([P, C], BF16, name="x_grouped", align_bytes=64, bufs=2)
+            x_grouped[m] = grouped
+            for pair in range(PASSES // 2):
+                bank = psum.tile([P, N_TILE], F32, name="bank")
+                for gi in range(2):
+                    g = 2 * pair + gi
+                    for u in range(2):
+                        slot = 2 * gi + u
+                        nc.tensor.transpose(
+                            bank[:, slot * P : (slot + 1) * P],
+                            words[:, 256 * g + u : 256 * (g + 1) : 2],
+                            ident[:],
+                        )
+                nc.scalar.copy(
+                    out=grouped[:].bitcast(F32)[:, pair * N_TILE : (pair + 1) * N_TILE].rearrange(
+                        "p (g r u) -> p g r u", g=2, u=2
+                    ),
+                    in_=bank[:].rearrange("p (g u r) -> p g r u", g=2, u=2),
+                )
+
+        def quantize_x(m):
+            nc.vector.quantize_mx(
+                out=x_codes[:, m, :].bitcast(E5M2X4), scales=x_scales[:, m, :], in_=x_grouped[m][:]
+            )
+
+        w_grouped = {}
+        w_codes = {}
+        w_scales = {}
+
+        def interleave(u):
+            cv = vector_columns(u)
+            grouped = grp.tile([P, N_TILE, PACK], BF16, name="w_grouped", align_bytes=64)
+            src = w_raw[u][:].rearrange("p j w -> p w j")
+            nc.vector.tensor_copy(out=grouped[:, 0:cv, :], in_=src[:, 0:cv, :])
+            nc.scalar.copy(out=grouped[:, cv:N_TILE, :], in_=src[:, cv:N_TILE, :])
+            w_grouped[u] = grouped
+
+        def quantize_w(u):
+            codes = wcp.tile([P, N_TILE], U32, name="w_codes", align_bytes=64)
+            scales = wcp.tile([P, N_TILE], U8, name="w_scales", align_bytes=64)
+            nc.vector.quantize_mx(
+                out=codes[:].bitcast(E5M2X4),
+                scales=scales[:],
+                in_=w_grouped[u][:].rearrange("p w j -> p (w j)"),
+            )
+            w_codes[u] = codes
+            w_scales[u] = scales
+
+        acc = {}
+
+        def multiply(n, g, m):
+            u = n * PASSES + g
+            if g == 0:
+                acc[n * BATCH + m] = psum.tile([P, N_TILE], F32, name="bank")
+            tokens = slice(g * P, (g + 1) * P)
+            nc.tensor.matmul_mx(
+                out=acc[n * BATCH + m][:],
+                lhsT=x_codes[:, m, tokens].bitcast(E5M2X4),
+                lhsT_scale=x_scales[:, m, tokens],
+                rhs=w_codes[u][:].bitcast(E5M2X4),
+                rhs_scale=w_scales[u][:],
+                start=(g == 0),
+                stop=(g == PASSES - 1),
+            )
+
+        root = {}
+        rstd = {}
+        prod_a = {}
+        prod_b = {}
+        rotated = {}
+
+        def sum_squares(b):
+            ss = stat.tile([P, HEADS_PER_TILE], F32, name="ss")
+            for h in range(HEADS_PER_TILE):
+                junk = stat.tile([P, D], BF16, name="junk")
+                nc.scalar.activation(
+                    out=junk[:], in_=acc[b][:, h * D : (h + 1) * D], func=ACT.Square, accum_out=ss[:, h : h + 1]
+                )
+            root[b] = stat.tile([P, HEADS_PER_TILE], F32, name="root")
+            nc.scalar.activation(out=root[b][:], in_=ss[:], func=ACT.Sqrt, bias=eps[:], scale=1.0 / D)
+
+        def products(b):
+            q = 1 if b < BATCH else 0
+            pa = epi.tile([P, N_TILE], F32, name="prod_a")
+            pb = epi.tile([P, N_TILE], F32, name="prod_b")
+            nc.vector.tensor_tensor(
+                out=pa[:].rearrange("p (h d) -> p h d", d=D),
+                in0=acc[b][:].rearrange("p (h d) -> p h d", d=D),
+                in1=tab_a[:, q : q + 1, :].to_broadcast([P, HEADS_PER_TILE, D]),
+                op=ALU.mult,
+            )
+            halves_in = acc[b][:].rearrange("p (h two e) -> p h two e", two=2, e=HALF)
+            halves_out = pb[:].rearrange("p (h two e) -> p h two e", two=2, e=HALF)
+            for half in range(2):
+                nc.vector.tensor_tensor(
+                    out=halves_out[:, :, half, :],
+                    in0=halves_in[:, :, 1 - half, :],
+                    in1=tab_b[:, q, half : half + 1, :].to_broadcast([P, HEADS_PER_TILE, HALF]),
+                    op=ALU.mult,
+                )
+            prod_a[b] = pa
+            prod_b[b] = pb
+
+        def combine(b):
+            rstd[b] = stat.tile([P, HEADS_PER_TILE], F32, name="rstd")
+            nc.vector.reciprocal(out=rstd[b][:], in_=root[b][:])
+            rotated[b] = epi.tile([P, N_TILE], F32, name="rotated")
+            nc.vector.tensor_tensor(out=rotated[b][:], in0=prod_a[b][:], in1=prod_b[b][:], op=ALU.add)
+
+        def scale_and_store(b):
+            n, m = divmod(b, BATCH)
+            result = outp.tile([P, N_TILE], F32, name="result")
+            for h in range(HEADS_PER_TILE):
+                cols = slice(h * D, (h + 1) * D)
+                nc.scalar.activation(
+                    out=result[:, cols], in_=rotated[b][:, cols], func=ACT.Copy, scale=rstd[b][:, h : h + 1]
+                )
+            if n == 0:
+                dst = out_1[m, :, :, :]
+            else:
+                dst = out_0[m, :, (n - 1) * HEADS_PER_TILE : n * HEADS_PER_TILE, :]
+            nc.sync.dma_start(out=dst.rearrange("t h d -> t (h d)"), in_=result[:])
+
+        for s in range(BANKS + 9):
+            if s + PREFETCH < UNITS:
+                load_unit(s + PREFETCH)
+            if s < UNITS:
+                interleave(s)
+            if s < BATCH:
+                transpose_x(s)
+            if s == 2:
+                build_tables()
+            if 1 <= s <= UNITS:
+                quantize_w(s - 1)
+            if 1 <= s <= BATCH:
+                quantize_x(s - 1)
+            if s == PASSES:
+                for m in range(BATCH):
+                    for g in range(PASSES):
+                        multiply(0, g, m)
+            if PASSES < s <= UNITS:
+                n, g = divmod(s - 1, PASSES)
+                for m in range(BATCH):
+                    multiply(n, g, m)
+            if 0 <= s - 5 < BANKS:
+                sum_squares(s - 5)
+            if 0 <= s - 6 < BANKS:
+                products(s - 6)
+            if 0 <= s - 7 < BANKS:
+                combine(s - 7)
+            if 0 <= s - 8 < BANKS:
+                scale_and_store(s - 8)

@@ -31,9 +31,7 @@ PREFETCH = 8
 def vector_columns(u):
     if u < 4:
         return 320
-    if u < 6:
-        return 256
-    return 192
+    return 304
 
 
 def tile_multiheadattention_pa_kernel(tc, x, cos, sin, wq, wk, q_norm_w, k_norm_w, out_0, out_1):
@@ -57,8 +55,9 @@ def tile_multiheadattention_pa_kernel(tc, x, cos, sin, wq, wk, q_norm_w, k_norm_
         ident = const.tile([P, P], F32, name="ident")
         eps = const.tile([P, 1], F32, name="eps")
         warm = const.tile([P, 1], F32, name="warm")
-        nc.gpsimd.memset(eps[:], RMS_EPS)
+        flag = const.tile([P, 1], U32, name="flag")
         nc.gpsimd.memset(gain_rows[:], 0.0)
+        nc.gpsimd.memset(eps[:], RMS_EPS)
         nc.gpsimd.memset(ones[:], 1.0)
         make_identity(nc, ident[:])
         nc.scalar.dma_start(out=gain_rows[0:1, 0:D], in_=q_norm_w.rearrange("(o d) -> o d", o=1))
@@ -94,10 +93,10 @@ def tile_multiheadattention_pa_kernel(tc, x, cos, sin, wq, wk, q_norm_w, k_norm_
 
         tab_a = const.tile([P, 2, D], F32, name="tab_a")
         tab_b = const.tile([P, 2, 2, HALF], F32, name="tab_b")
-        gain_bank = psum.tile([P, N_TILE], F32, name="bank")
-        nc.tensor.matmul(out=gain_bank[:, 0 : 2 * D], lhsT=ones[:], rhs=gain_rows[:], start=True, stop=True)
 
         def build_tables():
+            gain_bank = psum.tile([P, N_TILE], F32, name="bank")
+            nc.tensor.matmul(out=gain_bank[:, 0 : 2 * D], lhsT=ones[:], rhs=gain_rows[:], start=True, stop=True)
             gains = gain_bank[:, 0 : 2 * D]
             by_half = gains.rearrange("p (q two e) -> p q two e", q=2, two=2)
             nc.vector.tensor_tensor(
@@ -230,11 +229,13 @@ def tile_multiheadattention_pa_kernel(tc, x, cos, sin, wq, wk, q_norm_w, k_norm_
             prod_a[b] = pa
             prod_b[b] = pb
 
-        def combine(b):
+        def combine(b, after_unit):
             rstd[b] = stat.tile([P, HEADS_PER_TILE], F32, name="rstd")
             nc.vector.reciprocal(out=rstd[b][:], in_=root[b][:])
             rotated[b] = epi.tile([P, N_TILE], F32, name="rotated")
-            nc.vector.tensor_tensor(out=rotated[b][:], in0=prod_a[b][:], in1=prod_b[b][:], op=ALU.add)
+            if after_unit < UNITS:
+                nc.gpsimd.tensor_copy(out=flag[:], in_=w_codes[after_unit][:, 0:1])
+            nc.gpsimd.tensor_tensor(out=rotated[b][:], in0=prod_a[b][:], in1=prod_b[b][:], op=ALU.add)
 
         def scale_and_store(b):
             n, m = divmod(b, BATCH)
@@ -253,12 +254,12 @@ def tile_multiheadattention_pa_kernel(tc, x, cos, sin, wq, wk, q_norm_w, k_norm_
         for s in range(BANKS + 9):
             if s + PREFETCH < UNITS:
                 load_unit(s + PREFETCH)
+            if s == 2:
+                build_tables()
             if s < UNITS:
                 interleave(s)
             if s < BATCH:
                 transpose_x(s)
-            if s == 2:
-                build_tables()
             if 1 <= s <= UNITS:
                 quantize_w(s - 1)
             if 1 <= s <= BATCH:
@@ -276,6 +277,6 @@ def tile_multiheadattention_pa_kernel(tc, x, cos, sin, wq, wk, q_norm_w, k_norm_
             if 0 <= s - 6 < BANKS:
                 products(s - 6)
             if 0 <= s - 7 < BANKS:
-                combine(s - 7)
+                combine(s - 7, s - 1)
             if 0 <= s - 8 < BANKS:
                 scale_and_store(s - 8)

@@ -28,10 +28,12 @@ BANKS = COL_TILES * BATCH
 PREFETCH = 8
 
 
-def vector_columns(u):
+def column_shares(u):
     if u < 4:
-        return 320
-    return 304
+        return 0, 320, 192
+    if u < 7:
+        return 0, 288, 224
+    return 144, 120, 248
 
 
 def tile_multiheadattention_pa_kernel(tc, x, cos, sin, wq, wk, q_norm_w, k_norm_w, out_0, out_1):
@@ -55,7 +57,6 @@ def tile_multiheadattention_pa_kernel(tc, x, cos, sin, wq, wk, q_norm_w, k_norm_
         ident = const.tile([P, P], F32, name="ident")
         eps = const.tile([P, 1], F32, name="eps")
         warm = const.tile([P, 1], F32, name="warm")
-        flag = const.tile([P, 1], U32, name="flag")
         nc.gpsimd.memset(gain_rows[:], 0.0)
         nc.gpsimd.memset(eps[:], RMS_EPS)
         nc.gpsimd.memset(ones[:], 1.0)
@@ -155,13 +156,25 @@ def tile_multiheadattention_pa_kernel(tc, x, cos, sin, wq, wk, q_norm_w, k_norm_
         w_codes = {}
         w_scales = {}
 
+        def interleave_early(u):
+            cg = column_shares(u)[0]
+            w_grouped[u] = grp.tile([P, N_TILE, PACK], BF16, name="w_grouped", align_bytes=64, bufs=2)
+            if cg > 0:
+                nc.gpsimd.tensor_scalar(
+                    out=w_grouped[u][:, 0:cg, :],
+                    in0=w_raw[u][:].rearrange("p j w -> p w j")[:, 0:cg, :],
+                    scalar1=1.0,
+                    scalar2=0.0,
+                    op0=ALU.mult,
+                    op1=ALU.add,
+                )
+
         def interleave(u):
-            cv = vector_columns(u)
-            grouped = grp.tile([P, N_TILE, PACK], BF16, name="w_grouped", align_bytes=64)
+            cg, cv = column_shares(u)[0:2]
+            grouped = w_grouped[u]
             src = w_raw[u][:].rearrange("p j w -> p w j")
-            nc.vector.tensor_copy(out=grouped[:, 0:cv, :], in_=src[:, 0:cv, :])
-            nc.scalar.copy(out=grouped[:, cv:N_TILE, :], in_=src[:, cv:N_TILE, :])
-            w_grouped[u] = grouped
+            nc.vector.tensor_copy(out=grouped[:, cg : cg + cv, :], in_=src[:, cg : cg + cv, :])
+            nc.scalar.copy(out=grouped[:, cg + cv : N_TILE, :], in_=src[:, cg + cv : N_TILE, :])
 
         def quantize_w(u):
             codes = wcp.tile([P, N_TILE], U32, name="w_codes", align_bytes=64)
@@ -229,13 +242,12 @@ def tile_multiheadattention_pa_kernel(tc, x, cos, sin, wq, wk, q_norm_w, k_norm_
             prod_a[b] = pa
             prod_b[b] = pb
 
-        def combine(b, after_unit):
+        def combine(b, on_gpsimd):
             rstd[b] = stat.tile([P, HEADS_PER_TILE], F32, name="rstd")
             nc.vector.reciprocal(out=rstd[b][:], in_=root[b][:])
             rotated[b] = epi.tile([P, N_TILE], F32, name="rotated")
-            if after_unit < UNITS:
-                nc.gpsimd.tensor_copy(out=flag[:], in_=w_codes[after_unit][:, 0:1])
-            nc.gpsimd.tensor_tensor(out=rotated[b][:], in0=prod_a[b][:], in1=prod_b[b][:], op=ALU.add)
+            engine = nc.gpsimd if on_gpsimd else nc.vector
+            engine.tensor_tensor(out=rotated[b][:], in0=prod_a[b][:], in1=prod_b[b][:], op=ALU.add)
 
         def scale_and_store(b):
             n, m = divmod(b, BATCH)
@@ -251,6 +263,7 @@ def tile_multiheadattention_pa_kernel(tc, x, cos, sin, wq, wk, q_norm_w, k_norm_
                 dst = out_0[m, :, (n - 1) * HEADS_PER_TILE : n * HEADS_PER_TILE, :]
             nc.sync.dma_start(out=dst.rearrange("t h d -> t (h d)"), in_=result[:])
 
+        interleave_early(0)
         for s in range(BANKS + 9):
             if s + PREFETCH < UNITS:
                 load_unit(s + PREFETCH)
@@ -264,6 +277,8 @@ def tile_multiheadattention_pa_kernel(tc, x, cos, sin, wq, wk, q_norm_w, k_norm_
                 quantize_w(s - 1)
             if 1 <= s <= BATCH:
                 quantize_x(s - 1)
+            if s + 1 < UNITS:
+                interleave_early(s + 1)
             if s == PASSES:
                 for m in range(BATCH):
                     for g in range(PASSES):
@@ -277,6 +292,6 @@ def tile_multiheadattention_pa_kernel(tc, x, cos, sin, wq, wk, q_norm_w, k_norm_
             if 0 <= s - 6 < BANKS:
                 products(s - 6)
             if 0 <= s - 7 < BANKS:
-                combine(s - 7, s - 1)
+                combine(s - 7, s > UNITS)
             if 0 <= s - 8 < BANKS:
                 scale_and_store(s - 8)

@@ -26,6 +26,7 @@ COL_TILES = (H + KH) * D // N_TILE
 UNITS = COL_TILES * PASSES
 BANKS = COL_TILES * BATCH
 PREFETCH = 8
+RUN = 4
 
 
 def column_shares(u):
@@ -33,7 +34,7 @@ def column_shares(u):
         return 0, 320, 192
     if u < 7:
         return 0, 288, 224
-    return 144, 120, 248
+    return 128, 128, 256
 
 
 def tile_multiheadattention_pa_kernel(tc, x, cos, sin, wq, wk, q_norm_w, k_norm_w, out_0, out_1):
@@ -65,7 +66,7 @@ def tile_multiheadattention_pa_kernel(tc, x, cos, sin, wq, wk, q_norm_w, k_norm_
         nc.scalar.dma_start(out=gain_rows[0:1, D : 2 * D], in_=k_norm_w.rearrange("(o d) -> o d", o=1))
         nc.scalar.dma_start(out=cs[:, 0, :], in_=cos.rearrange("a t b e -> (a t) (b e)"))
         nc.scalar.dma_start(out=cs[:, 1, :], in_=sin.rearrange("a t b e -> (a t) (b e)"))
-        nc.scalar.activation(out=warm[:], in_=eps[:], func=ACT.Sqrt)
+        nc.scalar.activation(out=warm[:], in_=eps[:], func=ACT.Abs_reciprocal_sqrt)
 
         w_raw = {}
         x_raw = {}
@@ -171,10 +172,11 @@ def tile_multiheadattention_pa_kernel(tc, x, cos, sin, wq, wk, q_norm_w, k_norm_
 
         def interleave(u):
             cg, cv = column_shares(u)[0:2]
-            grouped = w_grouped[u]
-            src = w_raw[u][:].rearrange("p j w -> p w j")
-            nc.vector.tensor_copy(out=grouped[:, cg : cg + cv, :], in_=src[:, cg : cg + cv, :])
-            nc.scalar.copy(out=grouped[:, cg + cv : N_TILE, :], in_=src[:, cg + cv : N_TILE, :])
+            dst = w_grouped[u][:].rearrange("p (c i) j -> p c j i", i=RUN)
+            src = w_raw[u][:].rearrange("p j (c i) -> p c j i", i=RUN)
+            first, second = cg // RUN, (cg + cv) // RUN
+            nc.vector.tensor_copy(out=dst[:, first:second, :, :], in_=src[:, first:second, :, :])
+            nc.scalar.copy(out=dst[:, second:, :, :], in_=src[:, second:, :, :])
 
         def quantize_w(u):
             codes = wcp.tile([P, N_TILE], U32, name="w_codes", align_bytes=64)
@@ -204,7 +206,6 @@ def tile_multiheadattention_pa_kernel(tc, x, cos, sin, wq, wk, q_norm_w, k_norm_
                 stop=(g == PASSES - 1),
             )
 
-        root = {}
         rstd = {}
         prod_a = {}
         prod_b = {}
@@ -217,8 +218,10 @@ def tile_multiheadattention_pa_kernel(tc, x, cos, sin, wq, wk, q_norm_w, k_norm_
                 nc.scalar.activation(
                     out=junk[:], in_=acc[b][:, h * D : (h + 1) * D], func=ACT.Square, accum_out=ss[:, h : h + 1]
                 )
-            root[b] = stat.tile([P, HEADS_PER_TILE], F32, name="root")
-            nc.scalar.activation(out=root[b][:], in_=ss[:], func=ACT.Sqrt, bias=eps[:], scale=1.0 / D)
+            rstd[b] = stat.tile([P, HEADS_PER_TILE], F32, name="rstd")
+            nc.scalar.activation(
+                out=rstd[b][:], in_=ss[:], func=ACT.Abs_reciprocal_sqrt, bias=eps[:], scale=1.0 / D
+            )
 
         def products(b):
             q = 1 if b < BATCH else 0
@@ -243,8 +246,6 @@ def tile_multiheadattention_pa_kernel(tc, x, cos, sin, wq, wk, q_norm_w, k_norm_
             prod_b[b] = pb
 
         def combine(b, on_gpsimd):
-            rstd[b] = stat.tile([P, HEADS_PER_TILE], F32, name="rstd")
-            nc.vector.reciprocal(out=rstd[b][:], in_=root[b][:])
             rotated[b] = epi.tile([P, N_TILE], F32, name="rotated")
             engine = nc.gpsimd if on_gpsimd else nc.vector
             engine.tensor_tensor(out=rotated[b][:], in0=prod_a[b][:], in1=prod_b[b][:], op=ALU.add)

@@ -33,8 +33,8 @@ def column_shares(u):
     if u < 4:
         return 0, 320, 192
     if u < 7:
-        return 0, 288, 224
-    return 128, 128, 256
+        return 0, 256, 256
+    return 160, 0, 352
 
 
 def tile_multiheadattention_pa_kernel(tc, x, cos, sin, wq, wk, q_norm_w, k_norm_w, out_0, out_1):
@@ -175,7 +175,8 @@ def tile_multiheadattention_pa_kernel(tc, x, cos, sin, wq, wk, q_norm_w, k_norm_
             dst = w_grouped[u][:].rearrange("p (c i) j -> p c j i", i=RUN)
             src = w_raw[u][:].rearrange("p j (c i) -> p c j i", i=RUN)
             first, second = cg // RUN, (cg + cv) // RUN
-            nc.vector.tensor_copy(out=dst[:, first:second, :, :], in_=src[:, first:second, :, :])
+            if cv > 0:
+                nc.vector.tensor_copy(out=dst[:, first:second, :, :], in_=src[:, first:second, :, :])
             nc.scalar.copy(out=dst[:, second:, :, :], in_=src[:, second:, :, :])
 
         def quantize_w(u):
@@ -209,7 +210,6 @@ def tile_multiheadattention_pa_kernel(tc, x, cos, sin, wq, wk, q_norm_w, k_norm_
         rstd = {}
         prod_a = {}
         prod_b = {}
-        rotated = {}
 
         def sum_squares(b):
             ss = stat.tile([P, HEADS_PER_TILE], F32, name="ss")
@@ -227,37 +227,35 @@ def tile_multiheadattention_pa_kernel(tc, x, cos, sin, wq, wk, q_norm_w, k_norm_
             q = 1 if b < BATCH else 0
             pa = epi.tile([P, N_TILE], F32, name="prod_a")
             pb = epi.tile([P, N_TILE], F32, name="prod_b")
-            nc.vector.tensor_tensor(
-                out=pa[:].rearrange("p (h d) -> p h d", d=D),
-                in0=acc[b][:].rearrange("p (h d) -> p h d", d=D),
-                in1=tab_a[:, q : q + 1, :].to_broadcast([P, HEADS_PER_TILE, D]),
-                op=ALU.mult,
-            )
             halves_in = acc[b][:].rearrange("p (h two e) -> p h two e", two=2, e=HALF)
             halves_out = pb[:].rearrange("p (h two e) -> p h two e", two=2, e=HALF)
-            for half in range(2):
-                nc.vector.tensor_tensor(
-                    out=halves_out[:, :, half, :],
-                    in0=halves_in[:, :, 1 - half, :],
-                    in1=tab_b[:, q, half : half + 1, :].to_broadcast([P, HEADS_PER_TILE, HALF]),
-                    op=ALU.mult,
+            for h in range(HEADS_PER_TILE):
+                cols = slice(h * D, (h + 1) * D)
+                nc.vector.scalar_tensor_tensor(
+                    out=pa[:, cols],
+                    in0=acc[b][:, cols],
+                    scalar=rstd[b][:, h : h + 1],
+                    in1=tab_a[:, q, :],
+                    op0=ALU.mult,
+                    op1=ALU.mult,
                 )
+                for half in range(2):
+                    nc.vector.scalar_tensor_tensor(
+                        out=halves_out[:, h, half, :],
+                        in0=halves_in[:, h, 1 - half, :],
+                        scalar=rstd[b][:, h : h + 1],
+                        in1=tab_b[:, q, half, :],
+                        op0=ALU.mult,
+                        op1=ALU.mult,
+                    )
             prod_a[b] = pa
             prod_b[b] = pb
 
-        def combine(b, on_gpsimd):
-            rotated[b] = epi.tile([P, N_TILE], F32, name="rotated")
-            engine = nc.gpsimd if on_gpsimd else nc.vector
-            engine.tensor_tensor(out=rotated[b][:], in0=prod_a[b][:], in1=prod_b[b][:], op=ALU.add)
-
-        def scale_and_store(b):
+        def combine_and_store(b, on_gpsimd):
             n, m = divmod(b, BATCH)
             result = outp.tile([P, N_TILE], F32, name="result")
-            for h in range(HEADS_PER_TILE):
-                cols = slice(h * D, (h + 1) * D)
-                nc.scalar.activation(
-                    out=result[:, cols], in_=rotated[b][:, cols], func=ACT.Copy, scale=rstd[b][:, h : h + 1]
-                )
+            engine = nc.gpsimd if on_gpsimd else nc.vector
+            engine.tensor_tensor(out=result[:], in0=prod_a[b][:], in1=prod_b[b][:], op=ALU.add)
             if n == 0:
                 dst = out_1[m, :, :, :]
             else:
@@ -265,7 +263,7 @@ def tile_multiheadattention_pa_kernel(tc, x, cos, sin, wq, wk, q_norm_w, k_norm_
             nc.sync.dma_start(out=dst.rearrange("t h d -> t (h d)"), in_=result[:])
 
         interleave_early(0)
-        for s in range(BANKS + 9):
+        for s in range(BANKS + 7):
             if s + PREFETCH < UNITS:
                 load_unit(s + PREFETCH)
             if s == 2:
@@ -293,6 +291,4 @@ def tile_multiheadattention_pa_kernel(tc, x, cos, sin, wq, wk, q_norm_w, k_norm_
             if 0 <= s - 6 < BANKS:
                 products(s - 6)
             if 0 <= s - 7 < BANKS:
-                combine(s - 7, s > UNITS)
-            if 0 <= s - 8 < BANKS:
-                scale_and_store(s - 8)
+                combine_and_store(s - 7, UNITS < s < BANKS + 7 - 1)

@@ -93,33 +93,33 @@ def tile_multiheadattention_pa_kernel(tc, x, cos, sin, wq, wk, q_norm_w, k_norm_
         for u in range(BATCH, PREFETCH):
             load_unit(u)
 
-        tab_a = const.tile([P, 2, D], F32, name="tab_a")
-        tab_b = const.tile([P, 2, 2, HALF], F32, name="tab_b")
+        tab = const.tile([P, 2, 2, D], F32, name="tab")
 
         def build_tables():
             gain_bank = psum.tile([P, N_TILE], F32, name="bank")
             nc.tensor.matmul(out=gain_bank[:, 0 : 2 * D], lhsT=ones[:], rhs=gain_rows[:], start=True, stop=True)
             gains = gain_bank[:, 0 : 2 * D]
             by_half = gains.rearrange("p (q two e) -> p q two e", q=2, two=2)
+            for q in range(2):
+                nc.vector.tensor_tensor(
+                    out=tab[:, q, 0, :].rearrange("p (two e) -> p two e", two=2),
+                    in0=by_half[:, q, :, :],
+                    in1=cs[:, 0:1, :].to_broadcast([P, 2, HALF]),
+                    op=ALU.mult,
+                )
             nc.vector.tensor_tensor(
-                out=tab_a[:].rearrange("p q (two e) -> p (q two) e", two=2),
-                in0=gains.rearrange("p (f e) -> p f e", e=HALF),
-                in1=cs[:, 0:1, :].to_broadcast([P, 4, HALF]),
+                out=tab[:, :, 1, 0:HALF],
+                in0=by_half[:, :, 0, :],
+                in1=cs[:, 1:2, :].to_broadcast([P, 2, HALF]),
                 op=ALU.mult,
             )
             nc.vector.scalar_tensor_tensor(
-                out=tab_b[:, :, 0, :],
+                out=tab[:, :, 1, HALF:D],
                 in0=by_half[:, :, 1, :],
                 scalar=-1.0,
                 in1=cs[:, 1:2, :].to_broadcast([P, 2, HALF]),
                 op0=ALU.mult,
                 op1=ALU.mult,
-            )
-            nc.vector.tensor_tensor(
-                out=tab_b[:, :, 1, :],
-                in0=by_half[:, :, 0, :],
-                in1=cs[:, 1:2, :].to_broadcast([P, 2, HALF]),
-                op=ALU.mult,
             )
 
         x_codes = const.tile([P, BATCH, PASSES * P], U32, name="x_codes", align_bytes=64)
@@ -208,8 +208,7 @@ def tile_multiheadattention_pa_kernel(tc, x, cos, sin, wq, wk, q_norm_w, k_norm_
             )
 
         rstd = {}
-        prod_a = {}
-        prod_b = {}
+        prod = {}
 
         def sum_squares(b):
             ss = stat.tile([P, HEADS_PER_TILE], F32, name="ss")
@@ -225,37 +224,30 @@ def tile_multiheadattention_pa_kernel(tc, x, cos, sin, wq, wk, q_norm_w, k_norm_
 
         def products(b):
             q = 1 if b < BATCH else 0
-            pa = epi.tile([P, N_TILE], F32, name="prod_a")
-            pb = epi.tile([P, N_TILE], F32, name="prod_b")
-            halves_in = acc[b][:].rearrange("p (h two e) -> p h two e", two=2, e=HALF)
-            halves_out = pb[:].rearrange("p (h two e) -> p h two e", two=2, e=HALF)
+            pr = epi.tile([P, HEADS_PER_TILE, 2, D], F32, name="prod")
             for h in range(HEADS_PER_TILE):
-                cols = slice(h * D, (h + 1) * D)
+                head = acc[b][:, h * D : (h + 1) * D].rearrange("p (o d) -> p o d", o=1)
                 nc.vector.scalar_tensor_tensor(
-                    out=pa[:, cols],
-                    in0=acc[b][:, cols],
+                    out=pr[:, h, :, :],
+                    in0=head.to_broadcast([P, 2, D]),
                     scalar=rstd[b][:, h : h + 1],
-                    in1=tab_a[:, q, :],
+                    in1=tab[:, q, :, :],
                     op0=ALU.mult,
                     op1=ALU.mult,
                 )
-                for half in range(2):
-                    nc.vector.scalar_tensor_tensor(
-                        out=halves_out[:, h, half, :],
-                        in0=halves_in[:, h, 1 - half, :],
-                        scalar=rstd[b][:, h : h + 1],
-                        in1=tab_b[:, q, half, :],
-                        op0=ALU.mult,
-                        op1=ALU.mult,
-                    )
-            prod_a[b] = pa
-            prod_b[b] = pb
+            prod[b] = pr
 
         def combine_and_store(b, on_gpsimd):
             n, m = divmod(b, BATCH)
             result = outp.tile([P, N_TILE], F32, name="result")
             engine = nc.gpsimd if on_gpsimd else nc.vector
-            engine.tensor_tensor(out=result[:], in0=prod_a[b][:], in1=prod_b[b][:], op=ALU.add)
+            halves = prod[b][:].rearrange("p h a (two e) -> p h a two e", two=2)
+            engine.tensor_tensor(
+                out=result[:].rearrange("p (h two e) -> p h two e", two=2, e=HALF),
+                in0=halves[:, :, 0, :, :],
+                in1=halves[:, :, 1, ::-1, :],
+                op=ALU.add,
+            )
             if n == 0:
                 dst = out_1[m, :, :, :]
             else:

@@ -31,10 +31,12 @@ RUN = 4
 
 def column_shares(u):
     if u < 4:
-        return 0, 320, 192
+        return 0, 256, 128, 128
     if u < 7:
-        return 0, 256, 256
-    return 160, 0, 352
+        return 0, 192, 192, 128
+    if u < 9:
+        return 160, 0, 224, 128
+    return 160, 0, 96, 256
 
 
 def tile_multiheadattention_pa_kernel(tc, x, cos, sin, wq, wk, q_norm_w, k_norm_w, out_0, out_1):
@@ -46,21 +48,23 @@ def tile_multiheadattention_pa_kernel(tc, x, cos, sin, wq, wk, q_norm_w, k_norm_
         const = ctx.enter_context(tc.tile_pool(name="const", bufs=1))
         wraw = ctx.enter_context(tc.tile_pool(name="wraw", bufs=1))
         grp = ctx.enter_context(tc.tile_pool(name="grp", bufs=3))
-        wcp = ctx.enter_context(tc.tile_pool(name="wcp", bufs=6))
+        wcp = ctx.enter_context(tc.tile_pool(name="wcp", bufs=1))
         stat = ctx.enter_context(tc.tile_pool(name="stat", bufs=4))
         epi = ctx.enter_context(tc.tile_pool(name="epi", bufs=3))
         outp = ctx.enter_context(tc.tile_pool(name="outp", bufs=4))
-        psum = ctx.enter_context(tc.psum_pool(name="psum", bufs=8))
+        psum = ctx.enter_context(tc.psum_pool(name="psum", bufs=4))
 
         cs = const.tile([P, 2, HALF], BF16, name="cs")
         gain_rows = const.tile([P, 2 * D], BF16, name="gain_rows")
         ones = const.tile([P, P], BF16, name="ones")
         ident = const.tile([P, P], F32, name="ident")
+        ident_bf = const.tile([P, P], BF16, name="ident_bf")
         eps = const.tile([P, 1], F32, name="eps")
         warm = const.tile([P, 1], F32, name="warm")
         nc.gpsimd.memset(gain_rows[:], 0.0)
         nc.gpsimd.memset(eps[:], RMS_EPS)
         nc.gpsimd.memset(ones[:], 1.0)
+        make_identity(nc, ident_bf[:])
         make_identity(nc, ident[:])
         nc.scalar.dma_start(out=gain_rows[0:1, 0:D], in_=q_norm_w.rearrange("(o d) -> o d", o=1))
         nc.scalar.dma_start(out=gain_rows[0:1, D : 2 * D], in_=k_norm_w.rearrange("(o d) -> o d", o=1))
@@ -96,7 +100,7 @@ def tile_multiheadattention_pa_kernel(tc, x, cos, sin, wq, wk, q_norm_w, k_norm_
         tab = const.tile([P, 2, 2, D], F32, name="tab")
 
         def build_tables():
-            gain_bank = psum.tile([P, N_TILE], F32, name="bank")
+            gain_bank = psum.tile([P, N_TILE], F32, name="work")
             nc.tensor.matmul(out=gain_bank[:, 0 : 2 * D], lhsT=ones[:], rhs=gain_rows[:], start=True, stop=True)
             gains = gain_bank[:, 0 : 2 * D]
             by_half = gains.rearrange("p (q two e) -> p q two e", q=2, two=2)
@@ -131,7 +135,7 @@ def tile_multiheadattention_pa_kernel(tc, x, cos, sin, wq, wk, q_norm_w, k_norm_
             grouped = grp.tile([P, C], BF16, name="x_grouped", align_bytes=64, bufs=2)
             x_grouped[m] = grouped
             for pair in range(PASSES // 2):
-                bank = psum.tile([P, N_TILE], F32, name="bank")
+                bank = psum.tile([P, N_TILE], F32, name="work")
                 for gi in range(2):
                     g = 2 * pair + gi
                     for u in range(2):
@@ -170,18 +174,37 @@ def tile_multiheadattention_pa_kernel(tc, x, cos, sin, wq, wk, q_norm_w, k_norm_
                     op1=ALU.add,
                 )
 
+        w_bank = {}
+
+        def interleave_on_tensor(u):
+            width = column_shares(u)[3]
+            w_bank[u] = psum.tile([P, 2 * N_TILE], BF16, name="work")
+            for i in range(width // P):
+                cols = slice(N_TILE - width + i * P, N_TILE - width + (i + 1) * P)
+                nc.tensor.matmul(
+                    out=w_bank[u][:, i * N_TILE : (i + 1) * N_TILE].rearrange("p (w j) -> p w j", j=PACK),
+                    lhsT=ident_bf[:],
+                    rhs=w_raw[u][:, :, cols].rearrange("p j w -> p w j"),
+                    start=True,
+                    stop=True,
+                )
+
         def interleave(u):
-            cg, cv = column_shares(u)[0:2]
+            cg, cv, cs, ct = column_shares(u)
             dst = w_grouped[u][:].rearrange("p (c i) j -> p c j i", i=RUN)
             src = w_raw[u][:].rearrange("p j (c i) -> p c j i", i=RUN)
-            first, second = cg // RUN, (cg + cv) // RUN
+            first, second, third = cg // RUN, (cg + cv) // RUN, (cg + cv + cs) // RUN
+            nc.scalar.copy(
+                out=w_grouped[u][:, N_TILE - ct :, :].rearrange("p w j -> p (w j)"),
+                in_=w_bank[u][:, 0 : ct * PACK],
+            )
             if cv > 0:
                 nc.vector.tensor_copy(out=dst[:, first:second, :, :], in_=src[:, first:second, :, :])
-            nc.scalar.copy(out=dst[:, second:, :, :], in_=src[:, second:, :, :])
+            nc.scalar.copy(out=dst[:, second:third, :, :], in_=src[:, second:third, :, :])
 
         def quantize_w(u):
-            codes = wcp.tile([P, N_TILE], U32, name="w_codes", align_bytes=64)
-            scales = wcp.tile([P, N_TILE], U8, name="w_scales", align_bytes=64)
+            codes = wcp.tile([P, N_TILE], U32, name="w_codes%d" % u, align_bytes=64)
+            scales = wcp.tile([P, N_TILE], U8, name="w_scales%d" % u, align_bytes=64)
             nc.vector.quantize_mx(
                 out=codes[:].bitcast(E5M2X4),
                 scales=scales[:],
@@ -192,20 +215,21 @@ def tile_multiheadattention_pa_kernel(tc, x, cos, sin, wq, wk, q_norm_w, k_norm_
 
         acc = {}
 
-        def multiply(n, g, m):
-            u = n * PASSES + g
-            if g == 0:
-                acc[n * BATCH + m] = psum.tile([P, N_TILE], F32, name="bank")
-            tokens = slice(g * P, (g + 1) * P)
-            nc.tensor.matmul_mx(
-                out=acc[n * BATCH + m][:],
-                lhsT=x_codes[:, m, tokens].bitcast(E5M2X4),
-                lhsT_scale=x_scales[:, m, tokens],
-                rhs=w_codes[u][:].bitcast(E5M2X4),
-                rhs_scale=w_scales[u][:],
-                start=(g == 0),
-                stop=(g == PASSES - 1),
-            )
+        def fill(b):
+            n, m = divmod(b, BATCH)
+            acc[b] = psum.tile([P, N_TILE], F32, name="acc")
+            for g in range(PASSES):
+                u = n * PASSES + g
+                tokens = slice(g * P, (g + 1) * P)
+                nc.tensor.matmul_mx(
+                    out=acc[b][:],
+                    lhsT=x_codes[:, m, tokens].bitcast(E5M2X4),
+                    lhsT_scale=x_scales[:, m, tokens],
+                    rhs=w_codes[u][:].bitcast(E5M2X4),
+                    rhs_scale=w_scales[u][:],
+                    start=(g == 0),
+                    stop=(g == PASSES - 1),
+                )
 
         rstd = {}
         prod = {}
@@ -255,6 +279,7 @@ def tile_multiheadattention_pa_kernel(tc, x, cos, sin, wq, wk, q_norm_w, k_norm_
             nc.sync.dma_start(out=dst.rearrange("t h d -> t (h d)"), in_=result[:])
 
         interleave_early(0)
+        interleave_on_tensor(0)
         for s in range(BANKS + 7):
             if s + PREFETCH < UNITS:
                 load_unit(s + PREFETCH)
@@ -264,20 +289,16 @@ def tile_multiheadattention_pa_kernel(tc, x, cos, sin, wq, wk, q_norm_w, k_norm_
                 interleave(s)
             if s < BATCH:
                 transpose_x(s)
+            if s + 1 < UNITS:
+                interleave_on_tensor(s + 1)
             if 1 <= s <= UNITS:
                 quantize_w(s - 1)
             if 1 <= s <= BATCH:
                 quantize_x(s - 1)
             if s + 1 < UNITS:
                 interleave_early(s + 1)
-            if s == PASSES:
-                for m in range(BATCH):
-                    for g in range(PASSES):
-                        multiply(0, g, m)
-            if PASSES < s <= UNITS:
-                n, g = divmod(s - 1, PASSES)
-                for m in range(BATCH):
-                    multiply(n, g, m)
+            if 0 <= s - 4 < BANKS:
+                fill(s - 4)
             if 0 <= s - 5 < BANKS:
                 sum_squares(s - 5)
             if 0 <= s - 6 < BANKS:

@@ -35,8 +35,8 @@ def column_shares(u):
     if u < 7:
         return 0, 192, 192, 128
     if u < 9:
-        return 160, 0, 224, 128
-    return 160, 0, 96, 256
+        return 128, 0, 256, 128
+    return 128, 0, 128, 256
 
 
 def tile_multiheadattention_pa_kernel(tc, x, cos, sin, wq, wk, q_norm_w, k_norm_w, out_0, out_1):

@@ -132,7 +132,7 @@ def tile_multiheadattention_pa_kernel(tc, x, cos, sin, wq, wk, q_norm_w, k_norm_
 
         def transpose_x(m):
             words = x_raw[m][:].bitcast(F32)
-            grouped = grp.tile([P, C], BF16, name="x_grouped", align_bytes=64, bufs=2)
+            grouped = grp.tile([P, C], BF16, name="x_grouped", align_bytes=64, bufs=3)
             x_grouped[m] = grouped
             for pair in range(PASSES // 2):
                 bank = psum.tile([P, N_TILE], F32, name="work")
@@ -163,7 +163,7 @@ def tile_multiheadattention_pa_kernel(tc, x, cos, sin, wq, wk, q_norm_w, k_norm_
 
         def interleave_early(u):
             cg = column_shares(u)[0]
-            w_grouped[u] = grp.tile([P, N_TILE, PACK], BF16, name="w_grouped", align_bytes=64, bufs=2)
+            w_grouped[u] = grp.tile([P, N_TILE, PACK], BF16, name="w_grouped", align_bytes=64, bufs=3)
             if cg > 0:
                 nc.gpsimd.tensor_scalar(
                     out=w_grouped[u][:, 0:cg, :],
@@ -279,6 +279,7 @@ def tile_multiheadattention_pa_kernel(tc, x, cos, sin, wq, wk, q_norm_w, k_norm_
             nc.sync.dma_start(out=dst.rearrange("t h d -> t (h d)"), in_=result[:])
 
         interleave_early(0)
+        interleave_early(1)
         interleave_on_tensor(0)
         for s in range(BANKS + 7):
             if s + PREFETCH < UNITS:
@@ -295,8 +296,8 @@ def tile_multiheadattention_pa_kernel(tc, x, cos, sin, wq, wk, q_norm_w, k_norm_
                 quantize_w(s - 1)
             if 1 <= s <= BATCH:
                 quantize_x(s - 1)
-            if s + 1 < UNITS:
-                interleave_early(s + 1)
+            if s + 2 < UNITS:
+                interleave_early(s + 2)
             if 0 <= s - 4 < BANKS:
                 fill(s - 4)
             if 0 <= s - 5 < BANKS:
@@ -304,4 +305,4 @@ def tile_multiheadattention_pa_kernel(tc, x, cos, sin, wq, wk, q_norm_w, k_norm_
             if 0 <= s - 6 < BANKS:
                 products(s - 6)
             if 0 <= s - 7 < BANKS:
-                combine_and_store(s - 7, UNITS < s < BANKS + 7 - 1)
+                combine_and_store(s - 7, UNITS < s < BANKS + 7 - 2)

@@ -194,13 +194,13 @@ def tile_multiheadattention_pa_kernel(tc, x, cos, sin, wq, wk, q_norm_w, k_norm_
             dst = w_grouped[u][:].rearrange("p (c i) j -> p c j i", i=RUN)
             src = w_raw[u][:].rearrange("p j (c i) -> p c j i", i=RUN)
             first, second, third = cg // RUN, (cg + cv) // RUN, (cg + cv + cs) // RUN
+            if cv > 0:
+                nc.vector.tensor_copy(out=dst[:, first:second, :, :], in_=src[:, first:second, :, :])
+            nc.scalar.copy(out=dst[:, second:third, :, :], in_=src[:, second:third, :, :])
             nc.scalar.copy(
                 out=w_grouped[u][:, N_TILE - ct :, :].rearrange("p w j -> p (w j)"),
                 in_=w_bank[u][:, 0 : ct * PACK],
             )
-            if cv > 0:
-                nc.vector.tensor_copy(out=dst[:, first:second, :, :], in_=src[:, first:second, :, :])
-            nc.scalar.copy(out=dst[:, second:third, :, :], in_=src[:, second:third, :, :])
 
         def quantize_w(u):
             codes = wcp.tile([P, N_TILE], U32, name="w_codes%d" % u, align_bytes=64)

from contextlib import ExitStack

import concourse.mybir as mybir
from concourse.masks import make_identity

BATCH, T, C, H, KH, D = 4, 128, 2048, 16, 4, 128
HALF = D // 2
RMS_EPS = 1e-6
FLOPS = 2 * BATCH * T * C * (H + KH) * D

F32 = mybir.dt.float32
BF16 = mybir.dt.bfloat16
U32 = mybir.dt.uint32
U8 = mybir.dt.uint8
E5M2X4 = mybir.dt.float8_e5m2_x4
ALU = mybir.AluOpType
ACT = mybir.ActivationFunctionType

P = 128
PACK = 4
K_PASS = P * PACK
PASSES = C // K_PASS
N_TILE = 512
HEADS_PER_TILE = N_TILE // D
COL_TILES = (H + KH) * D // N_TILE
UNITS = COL_TILES * PASSES
BANKS = COL_TILES * BATCH
PREFETCH = 8
RUN = 4


def column_shares(u):
    if u < 4:
        return 0, 256, 128, 128
    if u < 7:
        return 0, 192, 192, 128
    if u < 9:
        return 128, 0, 256, 128
    return 128, 0, 128, 256


def tile_multiheadattention_pa_kernel(tc, x, cos, sin, wq, wk, q_norm_w, k_norm_w, out_0, out_1):
    nc = tc.nc
    x_rows = x.flatten_outer_dims()

    with ExitStack() as ctx:
        ctx.enter_context(tc.manual_schedule())
        const = ctx.enter_context(tc.tile_pool(name="const", bufs=1))
        wraw = ctx.enter_context(tc.tile_pool(name="wraw", bufs=1))
        grp = ctx.enter_context(tc.tile_pool(name="grp", bufs=3))
        wcp = ctx.enter_context(tc.tile_pool(name="wcp", bufs=1))
        stat = ctx.enter_context(tc.tile_pool(name="stat", bufs=4))
        epi = ctx.enter_context(tc.tile_pool(name="epi", bufs=3))
        outp = ctx.enter_context(tc.tile_pool(name="outp", bufs=4))
        psum = ctx.enter_context(tc.psum_pool(name="psum", bufs=4))

        cs = const.tile([P, 2, HALF], BF16, name="cs")
        gain_rows = const.tile([P, 2 * D], BF16, name="gain_rows")
        ones = const.tile([P, P], BF16, name="ones")
        ident = const.tile([P, P], F32, name="ident")
        ident_bf = const.tile([P, P], BF16, name="ident_bf")
        eps = const.tile([P, 1], F32, name="eps")
        warm = const.tile([P, 1], F32, name="warm")
        nc.gpsimd.memset(gain_rows[:], 0.0)
        nc.gpsimd.memset(eps[:], RMS_EPS)
        nc.gpsimd.memset(ones[:], 1.0)
        make_identity(nc, ident_bf[:])
        make_identity(nc, ident[:])
        nc.scalar.dma_start(out=gain_rows[0:1, 0:D], in_=q_norm_w.rearrange("(o d) -> o d", o=1))
        nc.scalar.dma_start(out=gain_rows[0:1, D : 2 * D], in_=k_norm_w.rearrange("(o d) -> o d", o=1))
        nc.scalar.dma_start(out=cs[:, 0, :], in_=cos.rearrange("a t b e -> (a t) (b e)"))
        nc.scalar.dma_start(out=cs[:, 1, :], in_=sin.rearrange("a t b e -> (a t) (b e)"))
        nc.scalar.activation(out=warm[:], in_=eps[:], func=ACT.Abs_reciprocal_sqrt)

        w_raw = {}
        x_raw = {}

        def load_unit(u):
            n, g = divmod(u, PASSES)
            rows = slice(g * K_PASS, (g + 1) * K_PASS)
            if n == 0:
                src = wk[rows, :]
            else:
                src = wq[rows, (n - 1) * N_TILE : n * N_TILE]
            raw = wraw.tile([P, PACK, N_TILE], BF16, name="w_raw%d" % u)
            nc.sync.dma_start(out=raw[:], in_=src.rearrange("(p j) w -> p j w", j=PACK))
            w_raw[u] = raw

        def load_x(m):
            raw = wraw.tile([P, C], BF16, name="x_raw%d" % m)
            nc.sync.dma_start(out=raw[:], in_=x_rows[m * P : (m + 1) * P, :])
            x_raw[m] = raw

        for m in range(BATCH):
            load_unit(m)
            load_x(m)
        for u in range(BATCH, PREFETCH):
            load_unit(u)

        tab = const.tile([P, 2, 2, D], F32, name="tab")

        def build_tables():
            gain_bank = psum.tile([P, N_TILE], F32, name="work")
            nc.tensor.matmul(out=gain_bank[:, 0 : 2 * D], lhsT=ones[:], rhs=gain_rows[:], start=True, stop=True)
            gains = gain_bank[:, 0 : 2 * D]
            by_half = gains.rearrange("p (q two e) -> p q two e", q=2, two=2)
            for q in range(2):
                nc.vector.tensor_tensor(
                    out=tab[:, q, 0, :].rearrange("p (two e) -> p two e", two=2),
                    in0=by_half[:, q, :, :],
                    in1=cs[:, 0:1, :].to_broadcast([P, 2, HALF]),
                    op=ALU.mult,
                )
            nc.vector.tensor_tensor(
                out=tab[:, :, 1, 0:HALF],
                in0=by_half[:, :, 0, :],
                in1=cs[:, 1:2, :].to_broadcast([P, 2, HALF]),
                op=ALU.mult,
            )
            nc.vector.scalar_tensor_tensor(
                out=tab[:, :, 1, HALF:D],
                in0=by_half[:, :, 1, :],
                scalar=-1.0,
                in1=cs[:, 1:2, :].to_broadcast([P, 2, HALF]),
                op0=ALU.mult,
                op1=ALU.mult,
            )

        x_codes = const.tile([P, BATCH, PASSES * P], U32, name="x_codes", align_bytes=64)
        x_scales = const.tile([P, BATCH, PASSES * P], U8, name="x_scales", align_bytes=64)
        x_grouped = {}

        def transpose_x(m):
            words = x_raw[m][:].bitcast(F32)
            grouped = grp.tile([P, C], BF16, name="x_grouped", align_bytes=64, bufs=3)
            x_grouped[m] = grouped
            for pair in range(PASSES // 2):
                bank = psum.tile([P, N_TILE], F32, name="work")
                for gi in range(2):
                    g = 2 * pair + gi
                    for u in range(2):
                        slot = 2 * gi + u
                        nc.tensor.transpose(
                            bank[:, slot * P : (slot + 1) * P],
                            words[:, 256 * g + u : 256 * (g + 1) : 2],
                            ident[:],
                        )
                nc.scalar.copy(
                    out=grouped[:].bitcast(F32)[:, pair * N_TILE : (pair + 1) * N_TILE].rearrange(
                        "p (g r u) -> p g r u", g=2, u=2
                    ),
                    in_=bank[:].rearrange("p (g u r) -> p g r u", g=2, u=2),
                )

        def quantize_x(m):
            nc.vector.quantize_mx(
                out=x_codes[:, m, :].bitcast(E5M2X4), scales=x_scales[:, m, :], in_=x_grouped[m][:]
            )

        w_grouped = {}
        w_codes = {}
        w_scales = {}

        def interleave_early(u):
            cg = column_shares(u)[0]
            w_grouped[u] = grp.tile([P, N_TILE, PACK], BF16, name="w_grouped", align_bytes=64, bufs=3)
            if cg > 0:
                nc.gpsimd.tensor_scalar(
                    out=w_grouped[u][:, 0:cg, :],
                    in0=w_raw[u][:].rearrange("p j w -> p w j")[:, 0:cg, :],
                    scalar1=1.0,
                    scalar2=0.0,
                    op0=ALU.mult,
                    op1=ALU.add,
                )

        w_bank = {}

        def interleave_on_tensor(u):
            width = column_shares(u)[3]
            w_bank[u] = psum.tile([P, 2 * N_TILE], BF16, name="work")
            for i in range(width // P):
                cols = slice(N_TILE - width + i * P, N_TILE - width + (i + 1) * P)
                nc.tensor.matmul(
                    out=w_bank[u][:, i * N_TILE : (i + 1) * N_TILE].rearrange("p (w j) -> p w j", j=PACK),
                    lhsT=ident_bf[:],
                    rhs=w_raw[u][:, :, cols].rearrange("p j w -> p w j"),
                    start=True,
                    stop=True,
                )

        def interleave(u):
            cg, cv, cs, ct = column_shares(u)
            dst = w_grouped[u][:].rearrange("p (c i) j -> p c j i", i=RUN)
            src = w_raw[u][:].rearrange("p j (c i) -> p c j i", i=RUN)
            first, second, third = cg // RUN, (cg + cv) // RUN, (cg + cv + cs) // RUN
            if cv > 0:
                nc.vector.tensor_copy(out=dst[:, first:second, :, :], in_=src[:, first:second, :, :])
            nc.scalar.copy(out=dst[:, second:third, :, :], in_=src[:, second:third, :, :])
            nc.scalar.copy(
                out=w_grouped[u][:, N_TILE - ct :, :].rearrange("p w j -> p (w j)"),
                in_=w_bank[u][:, 0 : ct * PACK],
            )

        def quantize_w(u):
            codes = wcp.tile([P, N_TILE], U32, name="w_codes%d" % u, align_bytes=64)
            scales = wcp.tile([P, N_TILE], U8, name="w_scales%d" % u, align_bytes=64)
            nc.vector.quantize_mx(
                out=codes[:].bitcast(E5M2X4),
                scales=scales[:],
                in_=w_grouped[u][:].rearrange("p w j -> p (w j)"),
            )
            w_codes[u] = codes
            w_scales[u] = scales

        acc = {}

        def fill(b):
            n, m = divmod(b, BATCH)
            acc[b] = psum.tile([P, N_TILE], F32, name="acc")
            for g in range(PASSES):
                u = n * PASSES + g
                tokens = slice(g * P, (g + 1) * P)
                nc.tensor.matmul_mx(
                    out=acc[b][:],
                    lhsT=x_codes[:, m, tokens].bitcast(E5M2X4),
                    lhsT_scale=x_scales[:, m, tokens],
                    rhs=w_codes[u][:].bitcast(E5M2X4),
                    rhs_scale=w_scales[u][:],
                    start=(g == 0),
                    stop=(g == PASSES - 1),
                )

        rstd = {}
        prod = {}

        def sum_squares(b):
            ss = stat.tile([P, HEADS_PER_TILE], F32, name="ss")
            for h in range(HEADS_PER_TILE):
                junk = stat.tile([P, D], BF16, name="junk")
                nc.scalar.activation(
                    out=junk[:], in_=acc[b][:, h * D : (h + 1) * D], func=ACT.Square, accum_out=ss[:, h : h + 1]
                )
            rstd[b] = stat.tile([P, HEADS_PER_TILE], F32, name="rstd")
            nc.scalar.activation(
                out=rstd[b][:], in_=ss[:], func=ACT.Abs_reciprocal_sqrt, bias=eps[:], scale=1.0 / D
            )

        def products(b):
            q = 1 if b < BATCH else 0
            pr = epi.tile([P, HEADS_PER_TILE, 2, D], F32, name="prod")
            for h in range(HEADS_PER_TILE):
                head = acc[b][:, h * D : (h + 1) * D].rearrange("p (o d) -> p o d", o=1)
                nc.vector.scalar_tensor_tensor(
                    out=pr[:, h, :, :],
                    in0=head.to_broadcast([P, 2, D]),
                    scalar=rstd[b][:, h : h + 1],
                    in1=tab[:, q, :, :],
                    op0=ALU.mult,
                    op1=ALU.mult,
                )
            prod[b] = pr

        def combine_and_store(b, on_gpsimd):
            n, m = divmod(b, BATCH)
            result = outp.tile([P, N_TILE], F32, name="result")
            engine = nc.gpsimd if on_gpsimd else nc.vector
            halves = prod[b][:].rearrange("p h a (two e) -> p h a two e", two=2)
            engine.tensor_tensor(
                out=result[:].rearrange("p (h two e) -> p h two e", two=2, e=HALF),
                in0=halves[:, :, 0, :, :],
                in1=halves[:, :, 1, ::-1, :],
                op=ALU.add,
            )
            if n == 0:
                dst = out_1[m, :, :, :]
            else:
                dst = out_0[m, :, (n - 1) * HEADS_PER_TILE : n * HEADS_PER_TILE, :]
            nc.sync.dma_start(out=dst.rearrange("t h d -> t (h d)"), in_=result[:])

        interleave_early(0)
        interleave_early(1)
        interleave_on_tensor(0)
        for s in range(BANKS + 7):
            if s + PREFETCH < UNITS:
                load_unit(s + PREFETCH)
            if s == 2:
                build_tables()
            if s < UNITS:
                interleave(s)
            if s < BATCH:
                transpose_x(s)
            if s + 1 < UNITS:
                interleave_on_tensor(s + 1)
            if 1 <= s <= UNITS:
                quantize_w(s - 1)
            if 1 <= s <= BATCH:
                quantize_x(s - 1)
            if s + 2 < UNITS:
                interleave_early(s + 2)
            if 0 <= s - 4 < BANKS:
                fill(s - 4)
            if 0 <= s - 5 < BANKS:
                sum_squares(s - 5)
            if 0 <= s - 6 < BANKS:
                products(s - 6)
            if 0 <= s - 7 < BANKS:
                combine_and_store(s - 7, UNITS < s < BANKS + 7 - 2)
